import numpy as np
import ml_dtypes


def mxq(x, axis, fmt="e4m3"):
    dtype, down = {"e4m3": (ml_dtypes.float8_e4m3fn, 7), "e5m2": (ml_dtypes.float8_e5m2, 14)}[fmt]
    v = np.moveaxis(np.asarray(x, np.float32).astype(ml_dtypes.bfloat16).astype(np.float64), axis, -1)
    blocks = v.reshape(v.shape[:-1] + (-1, 32))
    amax = np.abs(blocks).max(-1, keepdims=True)
    byte = np.maximum(np.where(amax > 0, np.frexp(amax)[1] - 1 + 127, 0) - down, 1)
    scale = np.exp2(byte - 127.0)
    codes = (blocks / scale).astype(np.float32).astype(dtype).astype(np.float64)
    return np.moveaxis((codes * scale).reshape(v.shape), -1, axis)


WIDE = False


def mx_kscale(k):
    if not WIDE:
        return np.ones(k)
    levels = np.array([10, -10, 5, -5, 0])
    if k % 512:
        return np.exp2(np.random.permutation(np.resize(levels, k // 32))).repeat(32)
    a = np.empty((k // 512, 16))
    for p in range(k // 512):
        a[p, :8] = np.random.permutation(np.resize(levels, 8))
        for g in range(8):
            far = levels[np.abs(levels - a[p, g]) >= 10]
            a[p, g + 8] = far[np.random.randint(len(far))]
    return np.exp2(a.ravel()).repeat(32)


BF16 = ml_dtypes.bfloat16


def bf(x):
    return np.asarray(x, np.float32).astype(BF16)


def f64(x):
    return np.asarray(x).astype(np.float64)


BS, DC, R, C = 8, 128, 32, 32
N = R * C
THRESH = 0.85


def setup_inputs():
    s = mx_kscale(N)
    u = s / s.min()
    g = 2.0 ** np.round(np.log2(u.mean()))
    seg = np.random.standard_normal((BS, DC, R, C)) * 0.1 * np.sqrt(N)
    W0 = f64(bf(np.random.random_sample((BS, N, N))))
    return {"seg": bf(seg * (g / u).reshape(1, 1, R, C)),
            "W": bf(np.where(W0 > THRESH, W0 * u, W0))}


def reference(seg, W):
    seg, W = f64(seg), f64(W)
    bs, d, r, c = seg.shape
    Wt = np.where(W > THRESH, W, 0.0)
    D = Wt / Wt.sum(axis=-1, keepdims=True)
    seg_flat = seg.reshape(bs, d, r * c)
    out = mxq(seg_flat, 2, "e4m3") @ mxq(D, 2, "e4m3").transpose(0, 2, 1)
    return out.reshape(bs, d, r, c)

@@ -1,0 +1,265 @@
+from contextlib import ExitStack
+
+import concourse.mybir as mybir
+from concourse.masks import make_identity
+
+BF16 = mybir.dt.bfloat16
+F32 = mybir.dt.float32
+U32 = mybir.dt.uint32
+U8 = mybir.dt.uint8
+FP8X4 = mybir.dt.float8_e4m3fn_x4
+ALU = mybir.AluOpType
+ACT = mybir.ActivationFunctionType
+
+BATCH = 8
+CHANNELS = 128
+N = 1024
+P = 128
+THRESHOLD = 0.85
+FLOPS = 2 * BATCH * CHANNELS * N * N
+
+PASSES = 2
+PACK = 4
+ROW_TILES = BATCH * N // P
+TILES_PER_BATCH = N // P
+LOAD_TILES = 4
+LOADS_AHEAD = 6
+
+GROUP_SIZES = [4] * 14 + [2] * 4
+
+REGROUP_LAG = 2
+QUANTISE_LAG = 3
+LEAVE_LAG = 1
+
+
+def make_groups():
+    groups = []
+    for size in GROUP_SIZES:
+        groups.append((sum(GROUP_SIZES[: len(groups)]), size))
+    return groups
+
+
+def invert_step(first, size):
+    return first + size
+
+
+def normalise_step(first, size, r):
+    return invert_step(first, size) + 1 + (r - first)
+
+
+def quantise_step(first, size):
+    return normalise_step(first, size, first + size - 1) + REGROUP_LAG + QUANTISE_LAG
+
+
+def normalised_on_scalar(r):
+    return r % 8 in (1, 3, 7) and r < ROW_TILES - 2 * TILES_PER_BATCH
+
+
+def regrouped_on_vector(r):
+    return r == ROW_TILES - 2
+
+
+def tile_regu_diff_t_kernel(tc, seg, W, out):
+    nc = tc.nc
+    seg_v = seg.rearrange("b d r c -> b d (r c)")
+    w_v = W.rearrange("b (j p) n -> b p j n", p=P)
+    out_v = out.rearrange("b d r c -> b d (r c)")
+    groups = make_groups()
+    group_of = {}
+    for first, size in groups:
+        for r in range(first, first + size):
+            group_of[r] = (first, size)
+    steps = quantise_step(*groups[-1]) + LEAVE_LAG + 1
+
+    with ExitStack() as ctx:
+        const = ctx.enter_context(tc.tile_pool(name="const", bufs=1))
+        wpool = ctx.enter_context(tc.tile_pool(name="wpool", bufs=LOADS_AHEAD))
+        dpool = ctx.enter_context(tc.tile_pool(name="dpool", bufs=4))
+        small = ctx.enter_context(tc.tile_pool(name="small", bufs=6))
+        gpool = ctx.enter_context(tc.tile_pool(name="gpool", bufs=5))
+        qpool = ctx.enter_context(tc.tile_pool(name="qpool", bufs=3))
+        opool = ctx.enter_context(tc.tile_pool(name="opool", bufs=3))
+        tpsum = ctx.enter_context(tc.psum_pool(name="tpsum", bufs=6))
+        apsum = ctx.enter_context(tc.psum_pool(name="apsum", bufs=2))
+
+        ident = const.tile([P, P], BF16)
+        make_identity(nc, ident[:])
+        ident_f32 = const.tile([P, P], F32)
+        make_identity(nc, ident_f32[:])
+
+        seg_sb = const.tile([P, BATCH, N], BF16)
+        seg_grouped = const.tile([P, BATCH, PASSES, CHANNELS, PACK], BF16, align_bytes=64)
+        seg_codes = const.tile([P, BATCH, PASSES, CHANNELS], U32, align_bytes=64)
+        seg_scales = const.tile([P, BATCH, PASSES, CHANNELS], U8, align_bytes=64)
+
+        w_tiles = {}
+        banks = {}
+        seg_banks = {}
+        d_tiles = {}
+        sums = {}
+        inverses = {}
+        grouped = {}
+        quantised = {}
+        products = {}
+        results = {}
+
+        def load_rows(r, count):
+            base = r - r % LOAD_TILES
+            if r == base:
+                w_tiles[base] = wpool.tile([P, LOAD_TILES, N], BF16, name="w_sb")
+            j = r % TILES_PER_BATCH
+            nc.sync.dma_start(
+                out=w_tiles[base][:, r - base : r - base + count, :],
+                in_=w_v[r // TILES_PER_BATCH][:, j : j + count, :],
+            )
+
+        def load_seg(b):
+            nc.sync.dma_start(out=seg_sb[:, b, :], in_=seg_v[b])
+
+        def transpose_seg(b):
+            words = seg_sb[:, b, :].bitcast(F32)
+            bank = tpsum.tile([P, PASSES * 2, CHANNELS], F32, name="bank")
+            for k in range(PASSES * 2):
+                word = 2 * P * (k // 2) + k % 2
+                nc.tensor.transpose(bank[:, k, :], words[:, word : word + 2 * P - 1 : 2], ident_f32[:])
+            seg_banks[b] = bank
+
+        def regroup_seg(b):
+            nc.scalar.copy(
+                out=seg_grouped[:, b]
+                .rearrange("p c d t -> p c (d t)")
+                .bitcast(F32)
+                .rearrange("p c (d u) -> p c d u", u=2),
+                in_=seg_banks[b][:].rearrange("p (c u) d -> p c d u", u=2),
+            )
+
+        def quantise_seg(b):
+            nc.vector.quantize_mx(
+                out=seg_codes[:, b].rearrange("p c d -> p (c d)").bitcast(FP8X4),
+                scales=seg_scales[:, b].rearrange("p c d -> p (c d)"),
+                in_=seg_grouped[:, b].rearrange("p c d t -> p (c d t)"),
+            )
+
+        def threshold_and_sum(r):
+            first, size = group_of[r]
+            if r == first:
+                d_tiles[first] = dpool.tile([P, size, N], BF16, name="d_sb")
+                sums[first] = small.tile([P, size], F32, name="sums")
+            rows = w_tiles[r - r % LOAD_TILES][:, r % LOAD_TILES, :]
+            nc.vector.scalar_tensor_tensor(
+                out=d_tiles[first][:, r - first, :],
+                in0=rows,
+                scalar=THRESHOLD,
+                in1=rows,
+                op0=ALU.is_gt,
+                op1=ALU.mult,
+                accum_out=sums[first][:, r - first : r - first + 1],
+            )
+
+        def invert_sums(first, size):
+            inverses[first] = small.tile([P, size], F32, name="rinv")
+            nc.vector.reciprocal(inverses[first][:], sums[first][:])
+
+        def normalise(r):
+            first = group_of[r][0]
+            rows = d_tiles[first][:, r - first, :]
+            inverse = inverses[first][:, r - first : r - first + 1]
+            if normalised_on_scalar(r):
+                nc.scalar.activation(out=rows, in_=rows, func=ACT.Copy, scale=inverse)
+            else:
+                nc.vector.tensor_scalar_mul(out=rows, in0=rows, scalar1=inverse)
+
+        def transpose_rows(r):
+            first = group_of[r][0]
+            bank = tpsum.tile([P, PASSES * PACK, P], BF16, name="bank")
+            for k in range(PASSES * PACK):
+                column = PACK * P * (k // PACK) + k % PACK
+                nc.tensor.transpose(
+                    bank[:, k, :], d_tiles[first][:, r - first, column : column + PACK * P - 3 : PACK], ident[:]
+                )
+            banks[r] = bank
+
+        def regroup(r):
+            first, size = group_of[r]
+            if r == first:
+                grouped[first] = gpool.tile([P, PASSES, size * P, PACK], BF16, name="grouped", align_bytes=64)
+            dst = grouped[first][:, :, (r - first) * P : (r - first + 1) * P, :]
+            src = banks[r][:].rearrange("p (c t) m -> p c m t", t=PACK)
+            if regrouped_on_vector(r):
+                nc.vector.tensor_copy(out=dst, in_=src)
+            else:
+                nc.scalar.copy(out=dst, in_=src)
+
+        def quantise(first, size):
+            codes = qpool.tile([P, PASSES * size * P], U32, name="codes", align_bytes=64)
+            scales = qpool.tile([P, PASSES * size * P], U8, name="scales", align_bytes=64)
+            nc.vector.quantize_mx(
+                out=codes[:].bitcast(FP8X4),
+                scales=scales[:],
+                in_=grouped[first][:].rearrange("p c m t -> p (c m t)"),
+            )
+            quantised[first] = (codes, scales)
+
+        def multiply(first, size):
+            b = first // TILES_PER_BATCH
+            codes, scales = quantised[first]
+            products[first] = apsum.tile([P, size * P], F32, name="acc")
+            for c in range(PASSES):
+                cols = slice(c * size * P, (c + 1) * size * P)
+                nc.tensor.matmul_mx(
+                    out=products[first][:],
+                    lhsT=seg_codes[:, b, c, :].bitcast(FP8X4),
+                    lhsT_scale=seg_scales[:, b, c, :],
+                    rhs=codes[:, cols].bitcast(FP8X4),
+                    rhs_scale=scales[:, cols],
+                    start=(c == 0),
+                    stop=(c == PASSES - 1),
+                )
+
+        def leave_psum(first, size):
+            results[first] = opool.tile([P, size * P], F32, name="o_sb")
+            nc.scalar.copy(out=results[first][:], in_=products[first][:])
+
+        def store(first, size):
+            column = (first % TILES_PER_BATCH) * P
+            nc.sync.dma_start(
+                out=out_v[first // TILES_PER_BATCH][:, column : column + size * P], in_=results[first][:]
+            )
+
+        with tc.manual_schedule():
+            for b in range(BATCH):
+                load_rows(b, 1)
+                load_seg(b)
+            for r in range(BATCH, LOADS_AHEAD * LOAD_TILES, LOAD_TILES):
+                load_rows(r, LOAD_TILES)
+
+            for s in range(steps):
+                refill = s + (LOADS_AHEAD - 1) * LOAD_TILES
+                if s > 0 and s % LOAD_TILES == 0 and refill < ROW_TILES:
+                    load_rows(refill, LOAD_TILES)
+                if s < ROW_TILES:
+                    threshold_and_sum(s)
+                for first, size in groups:
+                    if s == invert_step(first, size):
+                        invert_sums(first, size)
+                if 0 <= s - 3 < BATCH:
+                    quantise_seg(s - 3)
+                if s < BATCH:
+                    transpose_seg(s)
+                for r in range(ROW_TILES):
+                    if s == normalise_step(*group_of[r], r):
+                        normalise(r)
+                        transpose_rows(r)
+                if 0 <= s - 1 < BATCH:
+                    regroup_seg(s - 1)
+                for r in range(ROW_TILES):
+                    if s == normalise_step(*group_of[r], r) + REGROUP_LAG:
+                        regroup(r)
+                for first, size in groups:
+                    if s == quantise_step(first, size):
+                        quantise(first, size)
+                        multiply(first, size)
+                for first, size in groups:
+                    if s == quantise_step(first, size) + LEAVE_LAG:
+                        leave_psum(first, size)
+                        store(first, size)

@@ -52,7 +52,7 @@ def quantise_step(first, size):
 
 
 def normalised_on_scalar(r):
-    return r % 8 in (1, 3, 7) and r < ROW_TILES - 2 * TILES_PER_BATCH
+    return r % 4 != 0 and r < ROW_TILES - TILES_PER_BATCH
 
 
 def regrouped_on_vector(r):
@@ -82,8 +82,6 @@ def tile_regu_diff_t_kernel(tc, seg, W, out):
         tpsum = ctx.enter_context(tc.psum_pool(name="tpsum", bufs=6))
         apsum = ctx.enter_context(tc.psum_pool(name="apsum", bufs=2))
 
-        ident = const.tile([P, P], BF16)
-        make_identity(nc, ident[:])
         ident_f32 = const.tile([P, P], F32)
         make_identity(nc, ident_f32[:])
 
@@ -171,20 +169,25 @@ def tile_regu_diff_t_kernel(tc, seg, W, out):
 
         def transpose_rows(r):
             first = group_of[r][0]
-            bank = tpsum.tile([P, PASSES * PACK, P], BF16, name="bank")
-            for k in range(PASSES * PACK):
-                column = PACK * P * (k // PACK) + k % PACK
-                nc.tensor.transpose(
-                    bank[:, k, :], d_tiles[first][:, r - first, column : column + PACK * P - 3 : PACK], ident[:]
-                )
+            words = d_tiles[first][:, r - first, :].bitcast(F32)
+            bank = tpsum.tile([P, PASSES * 2, P], F32, name="bank")
+            for k in range(PASSES * 2):
+                word = 2 * P * (k // 2) + k % 2
+                nc.tensor.transpose(bank[:, k, :], words[:, word : word + 2 * P - 1 : 2], ident_f32[:])
             banks[r] = bank
 
         def regroup(r):
             first, size = group_of[r]
             if r == first:
                 grouped[first] = gpool.tile([P, PASSES, size * P, PACK], BF16, name="grouped", align_bytes=64)
-            dst = grouped[first][:, :, (r - first) * P : (r - first + 1) * P, :]
-            src = banks[r][:].rearrange("p (c t) m -> p c m t", t=PACK)
+            columns = slice((r - first) * P * PACK, (r - first + 1) * P * PACK)
+            dst = (
+                grouped[first][:]
+                .rearrange("p c m t -> p c (m t)")[:, :, columns]
+                .bitcast(F32)
+                .rearrange("p c (m u) -> p c m u", u=2)
+            )
+            src = banks[r][:].rearrange("p (c u) m -> p c m u", u=2)
             if regrouped_on_vector(r):
                 nc.vector.tensor_copy(out=dst, in_=src)
             else:

@@ -52,7 +52,7 @@ def quantise_step(first, size):
 
 
 def normalised_on_scalar(r):
-    return r % 4 != 0 and r < ROW_TILES - TILES_PER_BATCH
+    return r % 8 in (1, 2, 4, 5, 7) and r < ROW_TILES - TILES_PER_BATCH
 
 
 def regrouped_on_vector(r):
@@ -74,7 +74,7 @@ def tile_regu_diff_t_kernel(tc, seg, W, out):
     with ExitStack() as ctx:
         const = ctx.enter_context(tc.tile_pool(name="const", bufs=1))
         wpool = ctx.enter_context(tc.tile_pool(name="wpool", bufs=LOADS_AHEAD))
-        dpool = ctx.enter_context(tc.tile_pool(name="dpool", bufs=4))
+        dpool = ctx.enter_context(tc.tile_pool(name="dpool", bufs=6))
         small = ctx.enter_context(tc.tile_pool(name="small", bufs=6))
         gpool = ctx.enter_context(tc.tile_pool(name="gpool", bufs=5))
         qpool = ctx.enter_context(tc.tile_pool(name="qpool", bufs=3))

@@ -20,43 +20,26 @@ FLOPS = 2 * BATCH * CHANNELS * N * N
 
 PASSES = 2
 PACK = 4
+BLOCKS = N // 2 // P
 ROW_TILES = BATCH * N // P
 TILES_PER_BATCH = N // P
 LOAD_TILES = 4
-LOADS_AHEAD = 6
+LOADS_AHEAD = 8
 
-GROUP_SIZES = [4] * 14 + [2] * 4
-
-REGROUP_LAG = 2
-QUANTISE_LAG = 3
-LEAVE_LAG = 1
+GROUP_SIZES = [1, 1, 2] + [4] * 14 + [2, 1, 1]
+GROUPS = len(GROUP_SIZES)
 
 
-def make_groups():
-    groups = []
-    for size in GROUP_SIZES:
-        groups.append((sum(GROUP_SIZES[: len(groups)]), size))
-    return groups
+def tiles_masked(g):
+    return GROUP_SIZES[g] if g < GROUPS - 2 else 0
 
 
-def invert_step(first, size):
-    return first + size
+def tiles_summed_on_tensor(g):
+    return (0, 0, 1, 2, 3)[GROUP_SIZES[g]] if g < GROUPS - 2 else 0
 
 
-def normalise_step(first, size, r):
-    return invert_step(first, size) + 1 + (r - first)
-
-
-def quantise_step(first, size):
-    return normalise_step(first, size, first + size - 1) + REGROUP_LAG + QUANTISE_LAG
-
-
-def normalised_on_scalar(r):
-    return r % 8 in (1, 2, 4, 5, 7) and r < ROW_TILES - TILES_PER_BATCH
-
-
-def regrouped_on_vector(r):
-    return r == ROW_TILES - 2
+def normalised_on_scalar(g, j):
+    return False
 
 
 def tile_regu_diff_t_kernel(tc, seg, W, out):
@@ -64,26 +47,27 @@ def tile_regu_diff_t_kernel(tc, seg, W, out):
     seg_v = seg.rearrange("b d r c -> b d (r c)")
     w_v = W.rearrange("b (j p) n -> b p j n", p=P)
     out_v = out.rearrange("b d r c -> b d (r c)")
-    groups = make_groups()
-    group_of = {}
-    for first, size in groups:
-        for r in range(first, first + size):
-            group_of[r] = (first, size)
-    steps = quantise_step(*groups[-1]) + LEAVE_LAG + 1
+    firsts = [sum(GROUP_SIZES[:g]) for g in range(GROUPS)]
 
     with ExitStack() as ctx:
         const = ctx.enter_context(tc.tile_pool(name="const", bufs=1))
         wpool = ctx.enter_context(tc.tile_pool(name="wpool", bufs=LOADS_AHEAD))
-        dpool = ctx.enter_context(tc.tile_pool(name="dpool", bufs=6))
-        small = ctx.enter_context(tc.tile_pool(name="small", bufs=6))
-        gpool = ctx.enter_context(tc.tile_pool(name="gpool", bufs=5))
+        jpool = ctx.enter_context(tc.tile_pool(name="jpool", bufs=2))
+        mpool = ctx.enter_context(tc.tile_pool(name="mpool", bufs=2))
+        dpool = ctx.enter_context(tc.tile_pool(name="dpool", bufs=4))
+        tpool = ctx.enter_context(tc.tile_pool(name="tpool", bufs=2))
+        small = ctx.enter_context(tc.tile_pool(name="small", bufs=4))
+        gpool = ctx.enter_context(tc.tile_pool(name="gpool", bufs=3))
         qpool = ctx.enter_context(tc.tile_pool(name="qpool", bufs=3))
         opool = ctx.enter_context(tc.tile_pool(name="opool", bufs=3))
-        tpsum = ctx.enter_context(tc.psum_pool(name="tpsum", bufs=6))
+        tpsum = ctx.enter_context(tc.psum_pool(name="tpsum", bufs=5))
+        spsum = ctx.enter_context(tc.psum_pool(name="spsum", bufs=1))
         apsum = ctx.enter_context(tc.psum_pool(name="apsum", bufs=2))
 
         ident_f32 = const.tile([P, P], F32)
         make_identity(nc, ident_f32[:])
+        ones = const.tile([P, 1], BF16)
+        nc.gpsimd.memset(ones[:], 1.0)
 
         seg_sb = const.tile([P, BATCH, N], BF16)
         seg_grouped = const.tile([P, BATCH, PASSES, CHANNELS, PACK], BF16, align_bytes=64)
@@ -91,11 +75,15 @@ def tile_regu_diff_t_kernel(tc, seg, W, out):
         seg_scales = const.tile([P, BATCH, PASSES, CHANNELS], U8, align_bytes=64)
 
         w_tiles = {}
-        banks = {}
         seg_banks = {}
+        kept = {}
         d_tiles = {}
+        w_banks = {}
+        turned = {}
+        turned_sums = {}
         sums = {}
         inverses = {}
+        d_banks = {}
         grouped = {}
         quantised = {}
         products = {}
@@ -114,10 +102,10 @@ def tile_regu_diff_t_kernel(tc, seg, W, out):
         def load_seg(b):
             nc.sync.dma_start(out=seg_sb[:, b, :], in_=seg_v[b])
 
-        def transpose_seg(b):
+        def turn_seg(b):
             words = seg_sb[:, b, :].bitcast(F32)
-            bank = tpsum.tile([P, PASSES * 2, CHANNELS], F32, name="bank")
-            for k in range(PASSES * 2):
+            bank = tpsum.tile([P, BLOCKS, CHANNELS], F32, name="bank")
+            for k in range(BLOCKS):
                 word = 2 * P * (k // 2) + k % 2
                 nc.tensor.transpose(bank[:, k, :], words[:, word : word + 2 * P - 1 : 2], ident_f32[:])
             seg_banks[b] = bank
@@ -138,79 +126,131 @@ def tile_regu_diff_t_kernel(tc, seg, W, out):
                 in_=seg_grouped[:, b].rearrange("p c d t -> p (c d t)"),
             )
 
-        def threshold_and_sum(r):
-            first, size = group_of[r]
-            if r == first:
-                d_tiles[first] = dpool.tile([P, size, N], BF16, name="d_sb")
-                sums[first] = small.tile([P, size], F32, name="sums")
-            rows = w_tiles[r - r % LOAD_TILES][:, r % LOAD_TILES, :]
+        def rows_of(g, j, count):
+            r = firsts[g] + j
+            base = r - r % LOAD_TILES
+            return w_tiles[base][:, r - base : r - base + count, :].rearrange("p j n -> p (j n)")
+
+        def make_mask(g):
+            count = tiles_masked(g)
+            if count:
+                kept[g] = mpool.tile([P, count * N], BF16, name="mask")
+                nc.vector.tensor_single_scalar(
+                    out=kept[g][:], in_=rows_of(g, 0, count), scalar=THRESHOLD, op=ALU.is_gt
+                )
+
+        def apply_mask(g, j, count):
+            columns = slice(j * N, (j + count) * N)
+            nc.vector.tensor_tensor(
+                out=d_tiles[g][:, columns], in0=kept[g][:, columns], in1=rows_of(g, j, count), op=ALU.mult
+            )
+
+        def sum_on_scalar(g, j):
+            spare = jpool.tile([P, N], BF16, name="spare")
+            nc.scalar.activation(
+                out=spare[:],
+                in_=d_tiles[g][:, j * N : (j + 1) * N],
+                func=ACT.Copy,
+                accum_out=sums[g][:, j : j + 1],
+            )
+
+        def threshold_and_sum(g, j):
+            rows = rows_of(g, j, 1)
             nc.vector.scalar_tensor_tensor(
-                out=d_tiles[first][:, r - first, :],
+                out=d_tiles[g][:, j * N : (j + 1) * N],
                 in0=rows,
                 scalar=THRESHOLD,
                 in1=rows,
                 op0=ALU.is_gt,
                 op1=ALU.mult,
-                accum_out=sums[first][:, r - first : r - first + 1],
+                accum_out=sums[g][:, j : j + 1],
             )
 
-        def invert_sums(first, size):
-            inverses[first] = small.tile([P, size], F32, name="rinv")
-            nc.vector.reciprocal(inverses[first][:], sums[first][:])
+        def turn_for_sums(g, j, count):
+            for j in range(j, j + count):
+                words = d_tiles[g][:, j * N : (j + 1) * N].bitcast(F32)
+                bank = tpsum.tile([P, BLOCKS, P], F32, name="bank")
+                for k in range(BLOCKS):
+                    nc.tensor.transpose(bank[:, k, :], words[:, k * P : (k + 1) * P], ident_f32[:])
+                w_banks[g, j] = bank
 
-        def normalise(r):
-            first = group_of[r][0]
-            rows = d_tiles[first][:, r - first, :]
-            inverse = inverses[first][:, r - first : r - first + 1]
-            if normalised_on_scalar(r):
+        def leave_for_sums(g, j):
+            if j == 0:
+                turned[g] = tpool.tile([P, tiles_summed_on_tensor(g), BLOCKS * P], F32, name="turned")
+            nc.scalar.copy(out=turned[g][:, j, :], in_=w_banks[g, j][:].rearrange("p k m -> p (k m)"))
+
+        def sum_on_tensor(g):
+            count = tiles_summed_on_tensor(g)
+            if count:
+                turned_sums[g] = spsum.tile([P, count], F32, name="sums")
+            for j in range(count):
+                values = turned[g][:, j, :].bitcast(BF16).rearrange("p (k m e) -> p k m e", m=P, e=2)
+                for i in range(2 * BLOCKS):
+                    nc.tensor.matmul(
+                        turned_sums[g][:, j : j + 1],
+                        lhsT=values[:, i // 2, :, i % 2],
+                        rhs=ones[:],
+                        start=(i == 0),
+                        stop=(i == 2 * BLOCKS - 1),
+                    )
+
+        def invert(g):
+            count = tiles_summed_on_tensor(g)
+            if count < GROUP_SIZES[g]:
+                nc.vector.reciprocal(inverses[g][:, count:], sums[g][:, count:])
+
+        def invert_turned(g):
+            count = tiles_summed_on_tensor(g)
+            if count:
+                nc.vector.reciprocal(inverses[g][:, :count], turned_sums[g][:])
+
+        def normalise(g, j):
+            rows = d_tiles[g][:, j * N : (j + 1) * N]
+            inverse = inverses[g][:, j : j + 1]
+            if normalised_on_scalar(g, j):
                 nc.scalar.activation(out=rows, in_=rows, func=ACT.Copy, scale=inverse)
             else:
                 nc.vector.tensor_scalar_mul(out=rows, in0=rows, scalar1=inverse)
 
-        def transpose_rows(r):
-            first = group_of[r][0]
-            words = d_tiles[first][:, r - first, :].bitcast(F32)
-            bank = tpsum.tile([P, PASSES * 2, P], F32, name="bank")
-            for k in range(PASSES * 2):
+        def turn_rows(g, j):
+            words = d_tiles[g][:, j * N : (j + 1) * N].bitcast(F32)
+            bank = tpsum.tile([P, BLOCKS, P], F32, name="bank")
+            for k in range(BLOCKS):
                 word = 2 * P * (k // 2) + k % 2
                 nc.tensor.transpose(bank[:, k, :], words[:, word : word + 2 * P - 1 : 2], ident_f32[:])
-            banks[r] = bank
+            d_banks[g, j] = bank
 
-        def regroup(r):
-            first, size = group_of[r]
-            if r == first:
-                grouped[first] = gpool.tile([P, PASSES, size * P, PACK], BF16, name="grouped", align_bytes=64)
-            columns = slice((r - first) * P * PACK, (r - first + 1) * P * PACK)
-            dst = (
-                grouped[first][:]
-                .rearrange("p c m t -> p c (m t)")[:, :, columns]
-                .bitcast(F32)
-                .rearrange("p c (m u) -> p c m u", u=2)
+        def start_regroup(g):
+            size = GROUP_SIZES[g]
+            grouped[g] = gpool.tile([P, PASSES, size * P * PACK], BF16, name="grouped", align_bytes=64)
+
+        def regroup(g, j):
+            words = grouped[g][:].bitcast(F32)
+            nc.scalar.copy(
+                out=words[:, :, 2 * P * j : 2 * P * (j + 1)].rearrange("p c (m u) -> p c m u", u=2),
+                in_=d_banks[g, j][:].rearrange("p (c u) m -> p c m u", u=2),
             )
-            src = banks[r][:].rearrange("p (c u) m -> p c m u", u=2)
-            if regrouped_on_vector(r):
-                nc.vector.tensor_copy(out=dst, in_=src)
-            else:
-                nc.scalar.copy(out=dst, in_=src)
 
-        def quantise(first, size):
-            codes = qpool.tile([P, PASSES * size * P], U32, name="codes", align_bytes=64)
-            scales = qpool.tile([P, PASSES * size * P], U8, name="scales", align_bytes=64)
+        def quantise(g):
+            width = PASSES * GROUP_SIZES[g] * P
+            codes = qpool.tile([P, width], U32, name="codes", align_bytes=64)
+            scales = qpool.tile([P, width], U8, name="scales", align_bytes=64)
             nc.vector.quantize_mx(
                 out=codes[:].bitcast(FP8X4),
                 scales=scales[:],
-                in_=grouped[first][:].rearrange("p c m t -> p (c m t)"),
+                in_=grouped[g][:].rearrange("p c x -> p (c x)"),
             )
-            quantised[first] = (codes, scales)
+            quantised[g] = (codes, scales)
 
-        def multiply(first, size):
-            b = first // TILES_PER_BATCH
-            codes, scales = quantised[first]
-            products[first] = apsum.tile([P, size * P], F32, name="acc")
+        def multiply(g):
+            b = firsts[g] // TILES_PER_BATCH
+            width = GROUP_SIZES[g] * P
+            codes, scales = quantised[g]
+            products[g] = apsum.tile([P, width], F32, name="acc")
             for c in range(PASSES):
-                cols = slice(c * size * P, (c + 1) * size * P)
+                cols = slice(c * width, (c + 1) * width)
                 nc.tensor.matmul_mx(
-                    out=products[first][:],
+                    out=products[g][:],
                     lhsT=seg_codes[:, b, c, :].bitcast(FP8X4),
                     lhsT_scale=seg_scales[:, b, c, :],
                     rhs=codes[:, cols].bitcast(FP8X4),
@@ -219,50 +259,81 @@ def tile_regu_diff_t_kernel(tc, seg, W, out):
                     stop=(c == PASSES - 1),
                 )
 
-        def leave_psum(first, size):
-            results[first] = opool.tile([P, size * P], F32, name="o_sb")
-            nc.scalar.copy(out=results[first][:], in_=products[first][:])
+        def leave_psum(g):
+            results[g] = opool.tile([P, GROUP_SIZES[g] * P], F32, name="o_sb")
+            nc.scalar.copy(out=results[g][:], in_=products[g][:])
 
-        def store(first, size):
-            column = (first % TILES_PER_BATCH) * P
+        def store(g):
+            r = firsts[g]
+            column = (r % TILES_PER_BATCH) * P
             nc.sync.dma_start(
-                out=out_v[first // TILES_PER_BATCH][:, column : column + size * P], in_=results[first][:]
+                out=out_v[r // TILES_PER_BATCH][:, column : column + GROUP_SIZES[g] * P], in_=results[g][:]
             )
 
         with tc.manual_schedule():
-            for b in range(BATCH):
-                load_rows(b, 1)
+            load_rows(0, 1)
+            load_rows(1, 1)
+            load_seg(0)
+            load_rows(2, 1)
+            load_rows(3, 1)
+            load_seg(1)
+            for b in range(2, BATCH):
+                load_rows(LOAD_TILES * (b - 1), LOAD_TILES)
                 load_seg(b)
-            for r in range(BATCH, LOADS_AHEAD * LOAD_TILES, LOAD_TILES):
-                load_rows(r, LOAD_TILES)
+            loaded = LOAD_TILES * (BATCH - 1)
+            while loaded < LOADS_AHEAD * LOAD_TILES:
+                load_rows(loaded, LOAD_TILES)
+                loaded += LOAD_TILES
 
-            for s in range(steps):
-                refill = s + (LOADS_AHEAD - 1) * LOAD_TILES
-                if s > 0 and s % LOAD_TILES == 0 and refill < ROW_TILES:
-                    load_rows(refill, LOAD_TILES)
-                if s < ROW_TILES:
-                    threshold_and_sum(s)
-                for first, size in groups:
-                    if s == invert_step(first, size):
-                        invert_sums(first, size)
-                if 0 <= s - 3 < BATCH:
-                    quantise_seg(s - 3)
-                if s < BATCH:
-                    transpose_seg(s)
-                for r in range(ROW_TILES):
-                    if s == normalise_step(*group_of[r], r):
-                        normalise(r)
-                        transpose_rows(r)
-                if 0 <= s - 1 < BATCH:
-                    regroup_seg(s - 1)
-                for r in range(ROW_TILES):
-                    if s == normalise_step(*group_of[r], r) + REGROUP_LAG:
-                        regroup(r)
-                for first, size in groups:
-                    if s == quantise_step(first, size):
-                        quantise(first, size)
-                        multiply(first, size)
-                for first, size in groups:
-                    if s == quantise_step(first, size) + LEAVE_LAG:
-                        leave_psum(first, size)
-                        store(first, size)
+            make_mask(0)
+            for k in range(GROUPS + 3):
+                if 0 < k < GROUPS and firsts[k] % LOAD_TILES == 0 and loaded < ROW_TILES:
+                    load_rows(loaded, LOAD_TILES)
+                    loaded += LOAD_TILES
+                before = k - 1 if 0 <= k - 1 < GROUPS else None
+                if k < GROUPS:
+                    size = GROUP_SIZES[k]
+                    masked = tiles_masked(k)
+                    count = tiles_summed_on_tensor(k)
+                    early = min(masked, 2)
+                    d_tiles[k] = dpool.tile([P, size * N], BF16, name="d_sb")
+                    sums[k] = small.tile([P, size], F32, name="sums_sb")
+                    inverses[k] = small.tile([P, size], F32, name="rinv")
+                    if early:
+                        apply_mask(k, 0, early)
+                        turn_for_sums(k, 0, min(early, count))
+                if before is not None:
+                    invert(before)
+                    invert_turned(before)
+                if k < GROUPS:
+                    for j in range(early, masked):
+                        apply_mask(k, j, 1)
+                        turn_for_sums(k, j, 1 if j < count else 0)
+                    for j in range(count):
+                        leave_for_sums(k, j)
+                if k < BATCH:
+                    turn_seg(k)
+                    regroup_seg(k)
+                if k < GROUPS:
+                    for j in range(count, masked):
+                        sum_on_scalar(k, j)
+                    for j in range(masked, size):
+                        threshold_and_sum(k, j)
+                if before is not None:
+                    for j in range(GROUP_SIZES[before]):
+                        normalise(before, j)
+                        turn_rows(before, j)
+                    start_regroup(before)
+                    for j in range(GROUP_SIZES[before]):
+                        regroup(before, j)
+                if k < GROUPS:
+                    sum_on_tensor(k)
+                if k + 1 < GROUPS:
+                    make_mask(k + 1)
+                if 0 <= k - 2 < GROUPS:
+                    quantise(k - 2)
+                    multiply(k - 2)
+                    leave_psum(k - 2)
+                    store(k - 2)
+                if 0 <= k - 1 < BATCH:
+                    quantise_seg(k - 1)

@@ -26,7 +26,7 @@ TILES_PER_BATCH = N // P
 LOAD_TILES = 4
 LOADS_AHEAD = 8
 
-GROUP_SIZES = [1, 1, 2] + [4] * 14 + [2, 1, 1]
+GROUP_SIZES = [2, 2] + [4] * 14 + [2, 1, 1]
 GROUPS = len(GROUP_SIZES)
 
 
@@ -35,11 +35,7 @@ def tiles_masked(g):
 
 
 def tiles_summed_on_tensor(g):
-    return (0, 0, 1, 2, 3)[GROUP_SIZES[g]] if g < GROUPS - 2 else 0
-
-
-def normalised_on_scalar(g, j):
-    return False
+    return GROUP_SIZES[g] if g < GROUPS - 2 else 0
 
 
 def tile_regu_diff_t_kernel(tc, seg, W, out):
@@ -54,7 +50,8 @@ def tile_regu_diff_t_kernel(tc, seg, W, out):
         wpool = ctx.enter_context(tc.tile_pool(name="wpool", bufs=LOADS_AHEAD))
         jpool = ctx.enter_context(tc.tile_pool(name="jpool", bufs=2))
         mpool = ctx.enter_context(tc.tile_pool(name="mpool", bufs=2))
-        dpool = ctx.enter_context(tc.tile_pool(name="dpool", bufs=4))
+        dpool = ctx.enter_context(tc.tile_pool(name="dpool", bufs=3))
+        ppool = ctx.enter_context(tc.tile_pool(name="ppool", bufs=2))
         tpool = ctx.enter_context(tc.tile_pool(name="tpool", bufs=2))
         small = ctx.enter_context(tc.tile_pool(name="small", bufs=4))
         gpool = ctx.enter_context(tc.tile_pool(name="gpool", bufs=3))
@@ -83,6 +80,7 @@ def tile_regu_diff_t_kernel(tc, seg, W, out):
         turned_sums = {}
         sums = {}
         inverses = {}
+        parted = {}
         d_banks = {}
         grouped = {}
         quantised = {}
@@ -139,7 +137,15 @@ def tile_regu_diff_t_kernel(tc, seg, W, out):
                     out=kept[g][:], in_=rows_of(g, 0, count), scalar=THRESHOLD, op=ALU.is_gt
                 )
 
+        def open_group(g):
+            size = GROUP_SIZES[g]
+            d_tiles[g] = dpool.tile([P, size * N], BF16, name="d_sb")
+            sums[g] = small.tile([P, size], F32, name="sums_sb")
+            inverses[g] = small.tile([P, size], F32, name="rinv")
+
         def apply_mask(g, j, count):
+            if count <= 0:
+                return
             columns = slice(j * N, (j + count) * N)
             nc.vector.tensor_tensor(
                 out=d_tiles[g][:, columns], in0=kept[g][:, columns], in1=rows_of(g, j, count), op=ALU.mult
@@ -205,19 +211,17 @@ def tile_regu_diff_t_kernel(tc, seg, W, out):
                 nc.vector.reciprocal(inverses[g][:, :count], turned_sums[g][:])
 
         def normalise(g, j):
-            rows = d_tiles[g][:, j * N : (j + 1) * N]
-            inverse = inverses[g][:, j : j + 1]
-            if normalised_on_scalar(g, j):
-                nc.scalar.activation(out=rows, in_=rows, func=ACT.Copy, scale=inverse)
-            else:
-                nc.vector.tensor_scalar_mul(out=rows, in0=rows, scalar1=inverse)
+            if j == 0:
+                parted[g] = ppool.tile([P, GROUP_SIZES[g] * N], BF16, name="parted")
+            rows = d_tiles[g][:, j * N : (j + 1) * N].rearrange("p (x u e) -> p u x e", u=2, e=2)
+            dst = parted[g][:, j * N : (j + 1) * N].rearrange("p (u x e) -> p u x e", u=2, e=2)
+            nc.vector.tensor_scalar_mul(out=dst, in0=rows, scalar1=inverses[g][:, j : j + 1])
 
         def turn_rows(g, j):
-            words = d_tiles[g][:, j * N : (j + 1) * N].bitcast(F32)
+            words = parted[g][:, j * N : (j + 1) * N].bitcast(F32)
             bank = tpsum.tile([P, BLOCKS, P], F32, name="bank")
             for k in range(BLOCKS):
-                word = 2 * P * (k // 2) + k % 2
-                nc.tensor.transpose(bank[:, k, :], words[:, word : word + 2 * P - 1 : 2], ident_f32[:])
+                nc.tensor.transpose(bank[:, k, :], words[:, k * P : (k + 1) * P], ident_f32[:])
             d_banks[g, j] = bank
 
         def start_regroup(g):
@@ -228,7 +232,7 @@ def tile_regu_diff_t_kernel(tc, seg, W, out):
             words = grouped[g][:].bitcast(F32)
             nc.scalar.copy(
                 out=words[:, :, 2 * P * j : 2 * P * (j + 1)].rearrange("p c (m u) -> p c m u", u=2),
-                in_=d_banks[g, j][:].rearrange("p (c u) m -> p c m u", u=2),
+                in_=d_banks[g, j][:].rearrange("p (u c) m -> p c m u", u=2),
             )
 
         def quantise(g):
@@ -285,54 +289,55 @@ def tile_regu_diff_t_kernel(tc, seg, W, out):
                 load_rows(loaded, LOAD_TILES)
                 loaded += LOAD_TILES
 
-            make_mask(0)
-            for k in range(GROUPS + 3):
+            for k in range(-1, GROUPS + 2):
                 if 0 < k < GROUPS and firsts[k] % LOAD_TILES == 0 and loaded < ROW_TILES:
                     load_rows(loaded, LOAD_TILES)
                     loaded += LOAD_TILES
-                before = k - 1 if 0 <= k - 1 < GROUPS else None
-                if k < GROUPS:
-                    size = GROUP_SIZES[k]
-                    masked = tiles_masked(k)
-                    count = tiles_summed_on_tensor(k)
-                    early = min(masked, 2)
-                    d_tiles[k] = dpool.tile([P, size * N], BF16, name="d_sb")
-                    sums[k] = small.tile([P, size], F32, name="sums_sb")
-                    inverses[k] = small.tile([P, size], F32, name="rinv")
-                    if early:
-                        apply_mask(k, 0, early)
-                        turn_for_sums(k, 0, min(early, count))
-                if before is not None:
-                    invert(before)
-                    invert_turned(before)
-                if k < GROUPS:
-                    for j in range(early, masked):
-                        apply_mask(k, j, 1)
-                        turn_for_sums(k, j, 1 if j < count else 0)
-                    for j in range(count):
+                if 0 <= k < GROUPS:
+                    open_group(k)
+                    apply_mask(k, 0, min(tiles_masked(k), 2))
+                if 0 <= k < GROUPS:
+                    turn_for_sums(k, 0, min(tiles_summed_on_tensor(k), 2))
+                if 0 <= k - 1 < GROUPS:
+                    invert(k - 1)
+                if 0 <= k - 1 < GROUPS:
+                    invert_turned(k - 1)
+                if 0 <= k < GROUPS:
+                    apply_mask(k, 2, tiles_masked(k) - 2)
+                if 0 <= k < GROUPS:
+                    turn_for_sums(k, 2, tiles_summed_on_tensor(k) - 2)
+                if 0 <= k < GROUPS:
+                    for j in range(tiles_summed_on_tensor(k)):
                         leave_for_sums(k, j)
-                if k < BATCH:
+                if 0 <= k < BATCH:
                     turn_seg(k)
+                if 0 <= k < BATCH:
                     regroup_seg(k)
-                if k < GROUPS:
-                    for j in range(count, masked):
+                if 0 <= k < GROUPS:
+                    for j in range(tiles_summed_on_tensor(k), tiles_masked(k)):
                         sum_on_scalar(k, j)
-                    for j in range(masked, size):
+                if 0 <= k < GROUPS:
+                    for j in range(tiles_masked(k), GROUP_SIZES[k]):
                         threshold_and_sum(k, j)
-                if before is not None:
-                    for j in range(GROUP_SIZES[before]):
-                        normalise(before, j)
-                        turn_rows(before, j)
-                    start_regroup(before)
-                    for j in range(GROUP_SIZES[before]):
-                        regroup(before, j)
-                if k < GROUPS:
+                if 0 <= k - 1 < GROUPS:
+                    for j in range(GROUP_SIZES[k - 1]):
+                        normalise(k - 1, j)
+                if 0 <= k - 1 < GROUPS:
+                    for j in range(GROUP_SIZES[k - 1]):
+                        turn_rows(k - 1, j)
+                if 0 <= k - 1 < GROUPS:
+                    start_regroup(k - 1)
+                    for j in range(GROUP_SIZES[k - 1]):
+                        regroup(k - 1, j)
+                if 0 <= k < GROUPS:
                     sum_on_tensor(k)
-                if k + 1 < GROUPS:
+                if 0 <= k + 1 < GROUPS:
                     make_mask(k + 1)
                 if 0 <= k - 2 < GROUPS:
                     quantise(k - 2)
+                if 0 <= k - 2 < GROUPS:
                     multiply(k - 2)
+                if 0 <= k - 2 < GROUPS:
                     leave_psum(k - 2)
                     store(k - 2)
                 if 0 <= k - 1 < BATCH:

@@ -25,17 +25,26 @@ ROW_TILES = BATCH * N // P
 TILES_PER_BATCH = N // P
 LOAD_TILES = 4
 LOADS_AHEAD = 8
+SUM_COLUMNS = 12
 
-GROUP_SIZES = [2, 2] + [4] * 14 + [2, 1, 1]
+GROUP_SIZES = [2, 2] + [4] * 14 + [2, 2]
 GROUPS = len(GROUP_SIZES)
 
 
 def tiles_masked(g):
-    return GROUP_SIZES[g] if g < GROUPS - 2 else 0
+    return GROUP_SIZES[g] if g < GROUPS - 1 else 0
+
+
+def normalising_step(g):
+    return g + 1 if tiles_masked(g) else g
 
 
 def tiles_summed_on_tensor(g):
-    return GROUP_SIZES[g] if g < GROUPS - 2 else 0
+    return GROUP_SIZES[g] if g < GROUPS - 1 else 0
+
+
+def normalised_in(step):
+    return [g for g in range(GROUPS) if normalising_step(g) == step]
 
 
 def tile_regu_diff_t_kernel(tc, seg, W, out):
@@ -63,7 +72,7 @@ def tile_regu_diff_t_kernel(tc, seg, W, out):
 
         ident_f32 = const.tile([P, P], F32)
         make_identity(nc, ident_f32[:])
-        ones = const.tile([P, 1], BF16)
+        ones = const.tile([P, SUM_COLUMNS], BF16)
         nc.gpsimd.memset(ones[:], 1.0)
 
         seg_sb = const.tile([P, BATCH, N], BF16)
@@ -129,13 +138,12 @@ def tile_regu_diff_t_kernel(tc, seg, W, out):
             base = r - r % LOAD_TILES
             return w_tiles[base][:, r - base : r - base + count, :].rearrange("p j n -> p (j n)")
 
-        def make_mask(g):
-            count = tiles_masked(g)
-            if count:
-                kept[g] = mpool.tile([P, count * N], BF16, name="mask")
-                nc.vector.tensor_single_scalar(
-                    out=kept[g][:], in_=rows_of(g, 0, count), scalar=THRESHOLD, op=ALU.is_gt
-                )
+        def make_mask(g, j, count):
+            if j == 0:
+                kept[g] = mpool.tile([P, tiles_masked(g) * N], BF16, name="mask")
+            nc.vector.tensor_single_scalar(
+                out=kept[g][:, j * N : (j + count) * N], in_=rows_of(g, j, count), scalar=THRESHOLD, op=ALU.is_gt
+            )
 
         def open_group(g):
             size = GROUP_SIZES[g]
@@ -188,12 +196,12 @@ def tile_regu_diff_t_kernel(tc, seg, W, out):
         def sum_on_tensor(g):
             count = tiles_summed_on_tensor(g)
             if count:
-                turned_sums[g] = spsum.tile([P, count], F32, name="sums")
+                turned_sums[g] = spsum.tile([P, count, SUM_COLUMNS], F32, name="sums")
             for j in range(count):
                 values = turned[g][:, j, :].bitcast(BF16).rearrange("p (k m e) -> p k m e", m=P, e=2)
                 for i in range(2 * BLOCKS):
                     nc.tensor.matmul(
-                        turned_sums[g][:, j : j + 1],
+                        turned_sums[g][:, j, :],
                         lhsT=values[:, i // 2, :, i % 2],
                         rhs=ones[:],
                         start=(i == 0),
@@ -208,7 +216,7 @@ def tile_regu_diff_t_kernel(tc, seg, W, out):
         def invert_turned(g):
             count = tiles_summed_on_tensor(g)
             if count:
-                nc.vector.reciprocal(inverses[g][:, :count], turned_sums[g][:])
+                nc.vector.reciprocal(inverses[g][:, :count], turned_sums[g][:, :, 0])
 
         def normalise(g, j):
             if j == 0:
@@ -275,37 +283,32 @@ def tile_regu_diff_t_kernel(tc, seg, W, out):
             )
 
         with tc.manual_schedule():
-            load_rows(0, 1)
-            load_rows(1, 1)
+            for r in range(LOAD_TILES):
+                load_rows(r, 1)
+            load_rows(LOAD_TILES, 2)
             load_seg(0)
-            load_rows(2, 1)
-            load_rows(3, 1)
+            load_rows(LOAD_TILES + 2, 2)
             load_seg(1)
             for b in range(2, BATCH):
-                load_rows(LOAD_TILES * (b - 1), LOAD_TILES)
+                load_rows(LOAD_TILES * b, LOAD_TILES)
                 load_seg(b)
-            loaded = LOAD_TILES * (BATCH - 1)
+            loaded = LOAD_TILES * BATCH
             while loaded < LOADS_AHEAD * LOAD_TILES:
                 load_rows(loaded, LOAD_TILES)
                 loaded += LOAD_TILES
 
-            for k in range(-1, GROUPS + 2):
+            make_mask(0, 0, 1)
+            make_mask(0, 1, 1)
+            for k in range(GROUPS + 2):
                 if 0 < k < GROUPS and firsts[k] % LOAD_TILES == 0 and loaded < ROW_TILES:
                     load_rows(loaded, LOAD_TILES)
                     loaded += LOAD_TILES
                 if 0 <= k < GROUPS:
                     open_group(k)
-                    apply_mask(k, 0, min(tiles_masked(k), 2))
-                if 0 <= k < GROUPS:
-                    turn_for_sums(k, 0, min(tiles_summed_on_tensor(k), 2))
-                if 0 <= k - 1 < GROUPS:
-                    invert(k - 1)
-                if 0 <= k - 1 < GROUPS:
-                    invert_turned(k - 1)
-                if 0 <= k < GROUPS:
-                    apply_mask(k, 2, tiles_masked(k) - 2)
-                if 0 <= k < GROUPS:
-                    turn_for_sums(k, 2, tiles_summed_on_tensor(k) - 2)
+                    piece = 1 if k == 0 else 2
+                    for j in range(0, tiles_masked(k), piece):
+                        apply_mask(k, j, piece)
+                        turn_for_sums(k, j, piece)
                 if 0 <= k < GROUPS:
                     for j in range(tiles_summed_on_tensor(k)):
                         leave_for_sums(k, j)
@@ -319,20 +322,26 @@ def tile_regu_diff_t_kernel(tc, seg, W, out):
                 if 0 <= k < GROUPS:
                     for j in range(tiles_masked(k), GROUP_SIZES[k]):
                         threshold_and_sum(k, j)
-                if 0 <= k - 1 < GROUPS:
-                    for j in range(GROUP_SIZES[k - 1]):
-                        normalise(k - 1, j)
-                if 0 <= k - 1 < GROUPS:
-                    for j in range(GROUP_SIZES[k - 1]):
-                        turn_rows(k - 1, j)
-                if 0 <= k - 1 < GROUPS:
-                    start_regroup(k - 1)
-                    for j in range(GROUP_SIZES[k - 1]):
-                        regroup(k - 1, j)
+                if k == 1:
+                    make_mask(k + 1, 0, 2)
+                for g in normalised_in(k):
+                    invert(g)
+                    invert_turned(g)
+                if 0 <= k + 1 < GROUPS and tiles_masked(k + 1):
+                    done = 2 if k == 1 else 0
+                    make_mask(k + 1, done, tiles_masked(k + 1) - done)
+                for g in normalised_in(k):
+                    for j in range(GROUP_SIZES[g]):
+                        normalise(g, j)
+                for g in normalised_in(k):
+                    for j in range(GROUP_SIZES[g]):
+                        turn_rows(g, j)
+                for g in normalised_in(k):
+                    start_regroup(g)
+                    for j in range(GROUP_SIZES[g]):
+                        regroup(g, j)
                 if 0 <= k < GROUPS:
                     sum_on_tensor(k)
-                if 0 <= k + 1 < GROUPS:
-                    make_mask(k + 1)
                 if 0 <= k - 2 < GROUPS:
                     quantise(k - 2)
                 if 0 <= k - 2 < GROUPS:

from contextlib import ExitStack

import concourse.mybir as mybir
from concourse.masks import make_identity

BF16 = mybir.dt.bfloat16
F32 = mybir.dt.float32
U32 = mybir.dt.uint32
U8 = mybir.dt.uint8
FP8X4 = mybir.dt.float8_e4m3fn_x4
ALU = mybir.AluOpType
ACT = mybir.ActivationFunctionType

BATCH = 8
CHANNELS = 128
N = 1024
P = 128
THRESHOLD = 0.85
FLOPS = 2 * BATCH * CHANNELS * N * N

PASSES = 2
PACK = 4
BLOCKS = N // 2 // P
ROW_TILES = BATCH * N // P
TILES_PER_BATCH = N // P
LOAD_TILES = 4
LOADS_AHEAD = 8
SUM_COLUMNS = 12

GROUP_SIZES = [2, 2] + [4] * 14 + [2, 2]
GROUPS = len(GROUP_SIZES)


def tiles_masked(g):
    return GROUP_SIZES[g] if g < GROUPS - 1 else 0


def normalising_step(g):
    return g + 1 if tiles_masked(g) else g


def tiles_summed_on_tensor(g):
    return GROUP_SIZES[g] if g < GROUPS - 1 else 0


def normalised_in(step):
    return [g for g in range(GROUPS) if normalising_step(g) == step]


def tile_regu_diff_t_kernel(tc, seg, W, out):
    nc = tc.nc
    seg_v = seg.rearrange("b d r c -> b d (r c)")
    w_v = W.rearrange("b (j p) n -> b p j n", p=P)
    out_v = out.rearrange("b d r c -> b d (r c)")
    firsts = [sum(GROUP_SIZES[:g]) for g in range(GROUPS)]

    with ExitStack() as ctx:
        const = ctx.enter_context(tc.tile_pool(name="const", bufs=1))
        wpool = ctx.enter_context(tc.tile_pool(name="wpool", bufs=LOADS_AHEAD))
        jpool = ctx.enter_context(tc.tile_pool(name="jpool", bufs=2))
        mpool = ctx.enter_context(tc.tile_pool(name="mpool", bufs=2))
        dpool = ctx.enter_context(tc.tile_pool(name="dpool", bufs=3))
        ppool = ctx.enter_context(tc.tile_pool(name="ppool", bufs=2))
        tpool = ctx.enter_context(tc.tile_pool(name="tpool", bufs=2))
        small = ctx.enter_context(tc.tile_pool(name="small", bufs=4))
        gpool = ctx.enter_context(tc.tile_pool(name="gpool", bufs=3))
        qpool = ctx.enter_context(tc.tile_pool(name="qpool", bufs=3))
        opool = ctx.enter_context(tc.tile_pool(name="opool", bufs=3))
        tpsum = ctx.enter_context(tc.psum_pool(name="tpsum", bufs=5))
        spsum = ctx.enter_context(tc.psum_pool(name="spsum", bufs=1))
        apsum = ctx.enter_context(tc.psum_pool(name="apsum", bufs=2))

        ident_f32 = const.tile([P, P], F32)
        make_identity(nc, ident_f32[:])
        ones = const.tile([P, SUM_COLUMNS], BF16)
        nc.gpsimd.memset(ones[:], 1.0)

        seg_sb = const.tile([P, BATCH, N], BF16)
        seg_grouped = const.tile([P, BATCH, PASSES, CHANNELS, PACK], BF16, align_bytes=64)
        seg_codes = const.tile([P, BATCH, PASSES, CHANNELS], U32, align_bytes=64)
        seg_scales = const.tile([P, BATCH, PASSES, CHANNELS], U8, align_bytes=64)

        w_tiles = {}
        seg_banks = {}
        kept = {}
        d_tiles = {}
        w_banks = {}
        turned = {}
        turned_sums = {}
        sums = {}
        inverses = {}
        parted = {}
        d_banks = {}
        grouped = {}
        quantised = {}
        products = {}
        results = {}

        def load_rows(r, count):
            base = r - r % LOAD_TILES
            if r == base:
                w_tiles[base] = wpool.tile([P, LOAD_TILES, N], BF16, name="w_sb")
            j = r % TILES_PER_BATCH
            nc.sync.dma_start(
                out=w_tiles[base][:, r - base : r - base + count, :],
                in_=w_v[r // TILES_PER_BATCH][:, j : j + count, :],
            )

        def load_seg(b):
            nc.sync.dma_start(out=seg_sb[:, b, :], in_=seg_v[b])

        def turn_seg(b):
            words = seg_sb[:, b, :].bitcast(F32)
            bank = tpsum.tile([P, BLOCKS, CHANNELS], F32, name="bank")
            for k in range(BLOCKS):
                word = 2 * P * (k // 2) + k % 2
                nc.tensor.transpose(bank[:, k, :], words[:, word : word + 2 * P - 1 : 2], ident_f32[:])
            seg_banks[b] = bank

        def regroup_seg(b):
            nc.scalar.copy(
                out=seg_grouped[:, b]
                .rearrange("p c d t -> p c (d t)")
                .bitcast(F32)
                .rearrange("p c (d u) -> p c d u", u=2),
                in_=seg_banks[b][:].rearrange("p (c u) d -> p c d u", u=2),
            )

        def quantise_seg(b):
            nc.vector.quantize_mx(
                out=seg_codes[:, b].rearrange("p c d -> p (c d)").bitcast(FP8X4),
                scales=seg_scales[:, b].rearrange("p c d -> p (c d)"),
                in_=seg_grouped[:, b].rearrange("p c d t -> p (c d t)"),
            )

        def rows_of(g, j, count):
            r = firsts[g] + j
            base = r - r % LOAD_TILES
            return w_tiles[base][:, r - base : r - base + count, :].rearrange("p j n -> p (j n)")

        def make_mask(g, j, count):
            if j == 0:
                kept[g] = mpool.tile([P, tiles_masked(g) * N], BF16, name="mask")
            nc.vector.tensor_single_scalar(
                out=kept[g][:, j * N : (j + count) * N], in_=rows_of(g, j, count), scalar=THRESHOLD, op=ALU.is_gt
            )

        def open_group(g):
            size = GROUP_SIZES[g]
            d_tiles[g] = dpool.tile([P, size * N], BF16, name="d_sb")
            sums[g] = small.tile([P, size], F32, name="sums_sb")
            inverses[g] = small.tile([P, size], F32, name="rinv")

        def apply_mask(g, j, count):
            if count <= 0:
                return
            columns = slice(j * N, (j + count) * N)
            nc.vector.tensor_tensor(
                out=d_tiles[g][:, columns], in0=kept[g][:, columns], in1=rows_of(g, j, count), op=ALU.mult
            )

        def sum_on_scalar(g, j):
            spare = jpool.tile([P, N], BF16, name="spare")
            nc.scalar.activation(
                out=spare[:],
                in_=d_tiles[g][:, j * N : (j + 1) * N],
                func=ACT.Copy,
                accum_out=sums[g][:, j : j + 1],
            )

        def threshold_and_sum(g, j):
            rows = rows_of(g, j, 1)
            nc.vector.scalar_tensor_tensor(
                out=d_tiles[g][:, j * N : (j + 1) * N],
                in0=rows,
                scalar=THRESHOLD,
                in1=rows,
                op0=ALU.is_gt,
                op1=ALU.mult,
                accum_out=sums[g][:, j : j + 1],
            )

        def turn_for_sums(g, j, count):
            for j in range(j, j + count):
                words = d_tiles[g][:, j * N : (j + 1) * N].bitcast(F32)
                bank = tpsum.tile([P, BLOCKS, P], F32, name="bank")
                for k in range(BLOCKS):
                    nc.tensor.transpose(bank[:, k, :], words[:, k * P : (k + 1) * P], ident_f32[:])
                w_banks[g, j] = bank

        def leave_for_sums(g, j):
            if j == 0:
                turned[g] = tpool.tile([P, tiles_summed_on_tensor(g), BLOCKS * P], F32, name="turned")
            nc.scalar.copy(out=turned[g][:, j, :], in_=w_banks[g, j][:].rearrange("p k m -> p (k m)"))

        def sum_on_tensor(g):
            count = tiles_summed_on_tensor(g)
            if count:
                turned_sums[g] = spsum.tile([P, count, SUM_COLUMNS], F32, name="sums")
            for j in range(count):
                values = turned[g][:, j, :].bitcast(BF16).rearrange("p (k m e) -> p k m e", m=P, e=2)
                for i in range(2 * BLOCKS):
                    nc.tensor.matmul(
                        turned_sums[g][:, j, :],
                        lhsT=values[:, i // 2, :, i % 2],
                        rhs=ones[:],
                        start=(i == 0),
                        stop=(i == 2 * BLOCKS - 1),
                    )

        def invert(g):
            count = tiles_summed_on_tensor(g)
            if count < GROUP_SIZES[g]:
                nc.vector.reciprocal(inverses[g][:, count:], sums[g][:, count:])

        def invert_turned(g):
            count = tiles_summed_on_tensor(g)
            if count:
                nc.vector.reciprocal(inverses[g][:, :count], turned_sums[g][:, :, 0])

        def normalise(g, j):
            if j == 0:
                parted[g] = ppool.tile([P, GROUP_SIZES[g] * N], BF16, name="parted")
            rows = d_tiles[g][:, j * N : (j + 1) * N].rearrange("p (x u e) -> p u x e", u=2, e=2)
            dst = parted[g][:, j * N : (j + 1) * N].rearrange("p (u x e) -> p u x e", u=2, e=2)
            nc.vector.tensor_scalar_mul(out=dst, in0=rows, scalar1=inverses[g][:, j : j + 1])

        def turn_rows(g, j):
            words = parted[g][:, j * N : (j + 1) * N].bitcast(F32)
            bank = tpsum.tile([P, BLOCKS, P], F32, name="bank")
            for k in range(BLOCKS):
                nc.tensor.transpose(bank[:, k, :], words[:, k * P : (k + 1) * P], ident_f32[:])
            d_banks[g, j] = bank

        def start_regroup(g):
            size = GROUP_SIZES[g]
            grouped[g] = gpool.tile([P, PASSES, size * P * PACK], BF16, name="grouped", align_bytes=64)

        def regroup(g, j):
            words = grouped[g][:].bitcast(F32)
            nc.scalar.copy(
                out=words[:, :, 2 * P * j : 2 * P * (j + 1)].rearrange("p c (m u) -> p c m u", u=2),
                in_=d_banks[g, j][:].rearrange("p (u c) m -> p c m u", u=2),
            )

        def quantise(g):
            width = PASSES * GROUP_SIZES[g] * P
            codes = qpool.tile([P, width], U32, name="codes", align_bytes=64)
            scales = qpool.tile([P, width], U8, name="scales", align_bytes=64)
            nc.vector.quantize_mx(
                out=codes[:].bitcast(FP8X4),
                scales=scales[:],
                in_=grouped[g][:].rearrange("p c x -> p (c x)"),
            )
            quantised[g] = (codes, scales)

        def multiply(g):
            b = firsts[g] // TILES_PER_BATCH
            width = GROUP_SIZES[g] * P
            codes, scales = quantised[g]
            products[g] = apsum.tile([P, width], F32, name="acc")
            for c in range(PASSES):
                cols = slice(c * width, (c + 1) * width)
                nc.tensor.matmul_mx(
                    out=products[g][:],
                    lhsT=seg_codes[:, b, c, :].bitcast(FP8X4),
                    lhsT_scale=seg_scales[:, b, c, :],
                    rhs=codes[:, cols].bitcast(FP8X4),
                    rhs_scale=scales[:, cols],
                    start=(c == 0),
                    stop=(c == PASSES - 1),
                )

        def leave_psum(g):
            results[g] = opool.tile([P, GROUP_SIZES[g] * P], F32, name="o_sb")
            nc.scalar.copy(out=results[g][:], in_=products[g][:])

        def store(g):
            r = firsts[g]
            column = (r % TILES_PER_BATCH) * P
            nc.sync.dma_start(
                out=out_v[r // TILES_PER_BATCH][:, column : column + GROUP_SIZES[g] * P], in_=results[g][:]
            )

        with tc.manual_schedule():
            for r in range(LOAD_TILES):
                load_rows(r, 1)
            load_rows(LOAD_TILES, 2)
            load_seg(0)
            load_rows(LOAD_TILES + 2, 2)
            load_seg(1)
            for b in range(2, BATCH):
                load_rows(LOAD_TILES * b, LOAD_TILES)
                load_seg(b)
            loaded = LOAD_TILES * BATCH
            while loaded < LOADS_AHEAD * LOAD_TILES:
                load_rows(loaded, LOAD_TILES)
                loaded += LOAD_TILES

            make_mask(0, 0, 1)
            make_mask(0, 1, 1)
            for k in range(GROUPS + 2):
                if 0 < k < GROUPS and firsts[k] % LOAD_TILES == 0 and loaded < ROW_TILES:
                    load_rows(loaded, LOAD_TILES)
                    loaded += LOAD_TILES
                if 0 <= k < GROUPS:
                    open_group(k)
                    piece = 1 if k == 0 else 2
                    for j in range(0, tiles_masked(k), piece):
                        apply_mask(k, j, piece)
                        turn_for_sums(k, j, piece)
                if 0 <= k < GROUPS:
                    for j in range(tiles_summed_on_tensor(k)):
                        leave_for_sums(k, j)
                if 0 <= k < BATCH:
                    turn_seg(k)
                if 0 <= k < BATCH:
                    regroup_seg(k)
                if 0 <= k < GROUPS:
                    for j in range(tiles_summed_on_tensor(k), tiles_masked(k)):
                        sum_on_scalar(k, j)
                if 0 <= k < GROUPS:
                    for j in range(tiles_masked(k), GROUP_SIZES[k]):
                        threshold_and_sum(k, j)
                if k == 1:
                    make_mask(k + 1, 0, 2)
                for g in normalised_in(k):
                    invert(g)
                    invert_turned(g)
                if 0 <= k + 1 < GROUPS and tiles_masked(k + 1):
                    done = 2 if k == 1 else 0
                    make_mask(k + 1, done, tiles_masked(k + 1) - done)
                for g in normalised_in(k):
                    for j in range(GROUP_SIZES[g]):
                        normalise(g, j)
                for g in normalised_in(k):
                    for j in range(GROUP_SIZES[g]):
                        turn_rows(g, j)
                for g in normalised_in(k):
                    start_regroup(g)
                    for j in range(GROUP_SIZES[g]):
                        regroup(g, j)
                if 0 <= k < GROUPS:
                    sum_on_tensor(k)
                if 0 <= k - 2 < GROUPS:
                    quantise(k - 2)
                if 0 <= k - 2 < GROUPS:
                    multiply(k - 2)
                if 0 <= k - 2 < GROUPS:
                    leave_psum(k - 2)
                    store(k - 2)
                if 0 <= k - 1 < BATCH:
                    quantise_seg(k - 1)
